import numpy as np
import ml_dtypes


def mxq(x, axis, fmt="e4m3"):
    dtype, down = {"e4m3": (ml_dtypes.float8_e4m3fn, 7), "e5m2": (ml_dtypes.float8_e5m2, 14)}[fmt]
    v = np.moveaxis(np.asarray(x, np.float32).astype(ml_dtypes.bfloat16).astype(np.float64), axis, -1)
    blocks = v.reshape(v.shape[:-1] + (-1, 32))
    amax = np.abs(blocks).max(-1, keepdims=True)
    byte = np.maximum(np.where(amax > 0, np.frexp(amax)[1] - 1 + 127, 0) - down, 1)
    scale = np.exp2(byte - 127.0)
    codes = (blocks / scale).astype(np.float32).astype(dtype).astype(np.float64)
    return np.moveaxis((codes * scale).reshape(v.shape), -1, axis)


WIDE = False


def mx_kscale(k):
    if not WIDE:
        return np.ones(k)
    levels = np.array([10, -10, 5, -5, 0])
    a = np.random.permutation(np.resize(levels, k // 512 * 4)).reshape(k // 512, 4)
    idx = np.arange(k)
    return np.exp2(a[idx // 512, idx % 128 // 32])


BF16 = ml_dtypes.bfloat16


def bf(x):
    return np.asarray(x, np.float32).astype(BF16)


def f64(x):
    return np.asarray(x).astype(np.float64)


PAD_EPS = 1e-9
B, L, H, F = 2, 1024, 512, 2048


def setup_inputs():
    s, t = mx_kscale(H), mx_kscale(F)
    return {"x": bf(np.random.standard_normal((B, L, H)) * s),
            "padding": bf(np.random.randint(0, 2, (B, L))),
            "filter_weight": bf(np.random.standard_normal((H, F)) * 0.044 / s[:, None] * t),
            "filter_bias": bf(np.random.standard_normal(F) * 0.1 * t),
            "output_weight": bf(np.random.standard_normal((F, H)) * 0.022 / t[:, None]),
            "output_bias": bf(np.random.standard_normal(H) * 0.1)}


def reference(x, padding, filter_weight, filter_bias, output_weight, output_bias):
    nonpad = (f64(padding) < PAD_EPS)[..., None]
    h = (mxq(f64(x), 2, "e4m3") @ mxq(f64(filter_weight), 0, "e4m3")) + f64(filter_bias)
    out = (mxq(h, 2, "e4m3") @ mxq(f64(output_weight), 0, "e4m3")) + f64(output_bias)
    return np.where(nonpad, out, 0.0)

@@ -1,0 +1,233 @@
+from contextlib import ExitStack
+
+import concourse.mybir as mybir
+from concourse.masks import make_identity
+
+FLOPS = 2 * 2048 * 512 * 2048 * 2
+
+F32 = mybir.dt.float32
+BF16 = mybir.dt.bfloat16
+U32 = mybir.dt.uint32
+U8 = mybir.dt.uint8
+FP8X4 = mybir.dt.float8_e4m3fn_x4
+ALU = mybir.AluOpType
+ACT = mybir.ActivationFunctionType
+
+P = 128
+NTB = 4
+NG = 4
+
+
+def build(tc, x, padding, w1, b1, w2, b2, out, sched, manual=True, hp_bufs=4, hg_bufs=3, hc_bufs=8, ot_bufs=6):
+    nc = tc.nc
+    with ExitStack() as ctx:
+        if manual:
+            ctx.enter_context(tc.manual_schedule())
+        const = ctx.enter_context(tc.tile_pool(name="const", bufs=1))
+        raw = ctx.enter_context(tc.tile_pool(name="raw", bufs=1))
+        work = ctx.enter_context(tc.tile_pool(name="work", bufs=1))
+        psum = ctx.enter_context(tc.psum_pool(name="psum", bufs=1))
+
+        xv = x.flatten_outer_dims().rearrange("(p i) k -> p (i k)", i=16)
+        ov = out.flatten_outer_dims().rearrange("(p i) n -> p i n", i=16)
+        w1v = w1.rearrange("(u q e) f -> q u e f", u=2, e=2)
+        w2v = w2.rearrange("(g p t) n -> p g (t n)", g=NG, t=4)
+
+        x_raw = [raw.tile([P, 2048], BF16, name="x_raw%d" % i) for i in range(NTB)]
+        w1_raw = [raw.tile([P, 4, 512], BF16, name="w1_raw%d" % i) for i in range(NG)]
+        w2_raw = [raw.tile([P, 4, 512], BF16, name="w2_raw%d" % i) for i in range(NG)]
+
+        xc = const.tile([P, NTB, 512], U32, name="xc", align_bytes=64)
+        xs = const.tile([P, NTB, 512], U8, name="xs", align_bytes=64)
+        w1c = const.tile([P, NG, 512], U32, name="w1c", align_bytes=64)
+        w1s = const.tile([P, NG, 512], U8, name="w1s", align_bytes=64)
+        w2c = const.tile([P, NG, 512], U32, name="w2c", align_bytes=64)
+        w2s = const.tile([P, NG, 512], U8, name="w2s", align_bytes=64)
+
+        ident = const.tile([P, P], F32, name="ident")
+        ones = const.tile([P, P], BF16, name="ones")
+        b2row = const.tile([P, 512], BF16, name="b2row")
+        b2bc = const.tile([P, 512], BF16, name="b2bc")
+        b2m = const.tile([P, 16, 512], BF16, name="b2m")
+        b1t = const.tile([P, 16], BF16, name="b1t")
+        b1f = const.tile([P, 16], F32, name="b1f")
+        padt = const.tile([P, 16], BF16, name="padt")
+        keep = const.tile([P, 16], F32, name="keep")
+
+        st = {}
+
+        def copy_on(e, dst, src):
+            if e == "S":
+                nc.scalar.copy(out=dst, in_=src)
+            elif e == "V":
+                nc.vector.tensor_copy(out=dst, in_=src)
+            else:
+                nc.gpsimd.tensor_scalar(out=dst, in0=src, scalar1=1.0, scalar2=0.0, op0=ALU.mult, op1=ALU.add)
+
+        def op_load(what, i):
+            if what == "x":
+                nc.sync.dma_start(out=x_raw[i][:], in_=xv[:, 2048 * i:2048 * (i + 1)])
+            elif what == "w1":
+                for u in range(2):
+                    nc.sync.dma_start(out=w1_raw[i][:, 2 * u:2 * u + 2, :], in_=w1v[:, u, :, 512 * i:512 * (i + 1)])
+            else:
+                nc.sync.dma_start(out=w2_raw[i][:].rearrange("p t n -> p (t n)"), in_=w2v[:, i, :])
+
+        def op_consts():
+            nc.vector.memset(b2row[:], 0.0)
+            nc.vector.memset(ones[:], 1.0)
+            nc.scalar.dma_start(out=b2row[0:1, :], in_=b2.unsqueeze(0))
+            nc.scalar.dma_start(out=b1t[:].rearrange("p (g t) -> p g t", t=4), in_=b1.rearrange("(g p t) -> p g t", g=NG, t=4))
+            nc.scalar.dma_start(out=padt[:], in_=padding.rearrange("b (q i) -> (b q) i", i=16))
+            make_identity(nc, ident[:])
+
+        def op_small():
+            nc.vector.tensor_copy(out=b1f[:], in_=b1t[:])
+            nc.vector.tensor_scalar(out=keep[:], in0=padt[:], scalar1=1e-9, scalar2=None, op0=ALU.is_lt)
+
+        def op_b2mm():
+            ps = psum.tile([P, 512], F32, name="b2ps", tag="y3")
+            nc.tensor.matmul(out=ps[:], lhsT=ones[:], rhs=b2row[:], start=True, stop=True)
+            st["b2ps"] = ps
+
+        def op_b2ev(e="S"):
+            copy_on(e, b2bc[:], st["b2ps"][:])
+
+        def op_b2m(i, e="V"):
+            if e == "V":
+                nc.vector.tensor_scalar(out=b2m[:, i, :], in0=b2bc[:], scalar1=keep[:, i:i + 1], scalar2=None, op0=ALU.mult)
+            else:
+                nc.scalar.activation(out=b2m[:, i, :], in_=b2bc[:], func=ACT.Copy, scale=keep[:, i:i + 1])
+
+        def op_xt(tb, h):
+            xw = x_raw[tb][:].bitcast(F32)
+            ps = psum.tile([P, 2, 2, P], F32, name="xps%d" % h, tag="h%d" % h)
+            for a in range(2):
+                for u in range(2):
+                    lo = 256 * (2 * h + a) + 128 * u
+                    nc.tensor.transpose(ps[:, a, u, :], xw[:, lo:lo + 128], ident[:])
+            st["xps", tb, h] = ps
+
+        def op_xe(tb, h, e="S"):
+            if ("xg", tb) not in st:
+                st["xg", tb] = work.tile([P, 2048], BF16, name="xg", tag="xg", bufs=2, align_bytes=64)
+            gw = st["xg", tb][:].bitcast(F32).rearrange("p (h a r u) -> p h a r u", h=2, a=2, u=2)
+            copy_on(e, gw[:, h], st["xps", tb, h][:].rearrange("p a u r -> p a r u"))
+
+        def op_xq(tb):
+            nc.vector.quantize_mx(out=xc[:, tb, :].bitcast(FP8X4), scales=xs[:, tb, :], in_=st["xg", tb][:])
+
+        def op_w1rg(g, e="V"):
+            t = work.tile([P, 2048], BF16, name="w1g", tag="w1g", bufs=2, align_bytes=64)
+            copy_on(e, t[:].rearrange("p (t m j) -> p t m j", t=4, j=4),
+                    w1_raw[g][:].rearrange("p j (m t) -> p t m j", t=4))
+            st["w1g", g] = t
+
+        def op_w1q(g):
+            nc.vector.quantize_mx(out=w1c[:, g, :].bitcast(FP8X4), scales=w1s[:, g, :], in_=st["w1g", g][:])
+
+        def regroup(e, dst, src):
+            copy_on(e, dst.rearrange("p (c i t) -> p c t i", i=4, t=4), src.rearrange("p t (c i) -> p c t i", i=4))
+
+        def op_w2rg(g, e="V"):
+            t = work.tile([P, 2048], BF16, name="w2g", tag="w2g", bufs=2, align_bytes=64)
+            regroup(e, t[:], w2_raw[g][:])
+            st["w2g", g] = t
+
+        def op_w2q(g):
+            nc.vector.quantize_mx(out=w2c[:, g, :].bitcast(FP8X4), scales=w2s[:, g, :], in_=st["w2g", g][:])
+
+        def op_s1(u, t):
+            tb, g = divmod(u, NG)
+            ps = psum.tile([P, 512], F32, name="hps%d" % t, tag="h%d" % t)
+            nc.tensor.matmul_mx(out=ps[:], lhsT=w1c[:, g, 128 * t:128 * (t + 1)].bitcast(FP8X4),
+                                lhsT_scale=w1s[:, g, 128 * t:128 * (t + 1)],
+                                rhs=xc[:, tb, :].bitcast(FP8X4), rhs_scale=xs[:, tb, :], start=True, stop=True)
+            st["hps", u, t] = ps
+
+        def cols(hf):
+            return (0, 512) if hf is None else (256 * hf, 256 * (hf + 1))
+
+        def op_ev(u, t, hf=None):
+            g = u % NG
+            if ("hp", u) not in st:
+                st["hp", u] = work.tile([P, 4, 512], BF16, name="hp", tag="hp", bufs=hp_bufs)
+            lo, hi = cols(hf)
+            nc.scalar.activation(out=st["hp", u][:, t, lo:hi], in_=st["hps", u, t][:, lo:hi], func=ACT.Identity,
+                                 bias=b1f[:, 4 * g + t:4 * g + t + 1], scale=1.0)
+
+        def op_rg(u, hf=None, e="V"):
+            if ("hg", u) not in st:
+                st["hg", u] = work.tile([P, 2048], BF16, name="hg", tag="hg", bufs=hg_bufs, align_bytes=64)
+            lo, hi = cols(hf)
+            regroup(e, st["hg", u][:, 4 * lo:4 * hi], st["hp", u][:, :, lo:hi])
+
+        def op_hq(u, hf=None):
+            if ("hc", u) not in st:
+                st["hc", u] = (work.tile([P, 512], U32, name="hc", tag="hc", bufs=hc_bufs, align_bytes=64),
+                               work.tile([P, 512], U8, name="hs", tag="hs", bufs=hc_bufs, align_bytes=64))
+            hc, hs = st["hc", u]
+            lo, hi = cols(hf)
+            nc.vector.quantize_mx(out=hc[:, lo:hi].bitcast(FP8X4), scales=hs[:, lo:hi], in_=st["hg", u][:, 4 * lo:4 * hi])
+
+        def op_s2(u, a):
+            tb, g = divmod(u, NG)
+            hc, hs = st["hc", u]
+            if g == 0:
+                st["y", tb, a] = psum.tile([P, 512], F32, name="yps%d" % a, tag="y%d" % a)
+            nc.tensor.matmul_mx(out=st["y", tb, a][:], lhsT=hc[:, 128 * a:128 * (a + 1)].bitcast(FP8X4),
+                                lhsT_scale=hs[:, 128 * a:128 * (a + 1)],
+                                rhs=w2c[:, g, :].bitcast(FP8X4), rhs_scale=w2s[:, g, :],
+                                start=(g == 0), stop=(g == NG - 1))
+
+        def op_out(tb, a):
+            i = 4 * tb + a
+            ot = work.tile([P, 512], F32, name="ot", tag="ot", bufs=ot_bufs)
+            nc.vector.scalar_tensor_tensor(out=ot[:], in0=st["y", tb, a][:], scalar=keep[:, i:i + 1],
+                                           in1=b2m[:, i, :], op0=ALU.mult, op1=ALU.add)
+            nc.sync.dma_start(out=ov[:, i, :], in_=ot[:])
+
+        table = dict(load=op_load, consts=op_consts, small=op_small, b2mm=op_b2mm, b2ev=op_b2ev, b2m=op_b2m,
+                     xt=op_xt, xe=op_xe, xq=op_xq, w1rg=op_w1rg, w1q=op_w1q, w2rg=op_w2rg, w2q=op_w2q,
+                     s1=op_s1, ev=op_ev, rg=op_rg, hq=op_hq, s2=op_s2, out=op_out)
+        for o in sched:
+            table[o[0]](*o[1:])
+
+
+LOADS = [("w1", 0), ("x", 0), ("w1", 1), ("w2", 0), ("w1", 2), ("w2", 1), ("w1", 3), ("w2", 2), ("x", 1), ("w2", 3),
+         ("x", 2), ("x", 3)]
+ON_SCALAR = (("w1", 1), ("w1", 2))
+
+
+def natural():
+    s = [("consts",)] + [("load",) + l for l in LOADS] + [("small",), ("b2mm",), ("b2ev", "S")]
+
+    def wprep(w, g):
+        e = "S" if (w, g) in ON_SCALAR else "V"
+        return [(w + "rg", g, e), (w + "q", g)]
+
+    def xprep(tb):
+        return [("xt", tb, 0), ("xt", tb, 1), ("xe", tb, 0, "S"), ("xe", tb, 1, "S"), ("xq", tb)]
+
+    s += wprep("w1", 0) + xprep(0)
+    for u in range(16):
+        tb, g = divmod(u, 4)
+        s += [("s1", u, t) for t in range(4)]
+        if tb == 0 and g < 3:
+            s += wprep("w1", g + 1)
+        s += [("ev", u, t, None) for t in range(4)]
+        if g == 1 and tb < 3:
+            s += xprep(tb + 1)
+        if tb == 0:
+            s += wprep("w2", g)
+        s += [("rg", u, None, "V"), ("hq", u, None)]
+        if g == 2:
+            s += [("b2m", 4 * tb + a, "V") for a in range(4)]
+        s += [("s2", u, a) for a in range(4)]
+        if g == 3:
+            s += [("out", tb, a) for a in range(4)]
+    return s
+
+
+def tile_feedforwardnetwork_kernel(tc, x, padding, filter_weight, filter_bias, output_weight, output_bias, out):
+    build(tc, x, padding, filter_weight, filter_bias, output_weight, output_bias, out, natural(), manual=False)

@@ -16,13 +16,18 @@ ACT = mybir.ActivationFunctionType
 P = 128
 NTB = 4
 NG = 4
+NU = NTB * NG
+LAG2 = 4
+LOADS = (("w1", 0), ("x", 0), ("w1", 1), ("w2", 0), ("w1", 2), ("w2", 1), ("w1", 3), ("w2", 2), ("x", 1), ("w2", 3),
+         ("x", 2), ("x", 3))
+RG_ON_SCALAR = (14,)
+SPLIT = (15,)
 
 
-def build(tc, x, padding, w1, b1, w2, b2, out, sched, manual=True, hp_bufs=4, hg_bufs=3, hc_bufs=8, ot_bufs=6):
+def tile_feedforwardnetwork_kernel(tc, x, padding, w1, b1, w2, b2, out):
     nc = tc.nc
     with ExitStack() as ctx:
-        if manual:
-            ctx.enter_context(tc.manual_schedule())
+        ctx.enter_context(tc.manual_schedule())
         const = ctx.enter_context(tc.tile_pool(name="const", bufs=1))
         raw = ctx.enter_context(tc.tile_pool(name="raw", bufs=1))
         work = ctx.enter_context(tc.tile_pool(name="work", bufs=1))
@@ -59,12 +64,10 @@ def build(tc, x, padding, w1, b1, w2, b2, out, sched, manual=True, hp_bufs=4, hg
         def copy_on(e, dst, src):
             if e == "S":
                 nc.scalar.copy(out=dst, in_=src)
-            elif e == "V":
-                nc.vector.tensor_copy(out=dst, in_=src)
             else:
-                nc.gpsimd.tensor_scalar(out=dst, in0=src, scalar1=1.0, scalar2=0.0, op0=ALU.mult, op1=ALU.add)
+                nc.vector.tensor_copy(out=dst, in_=src)
 
-        def op_load(what, i):
+        def load(what, i):
             if what == "x":
                 nc.sync.dma_start(out=x_raw[i][:], in_=xv[:, 2048 * i:2048 * (i + 1)])
             elif what == "w1":
@@ -73,161 +76,162 @@ def build(tc, x, padding, w1, b1, w2, b2, out, sched, manual=True, hp_bufs=4, hg
             else:
                 nc.sync.dma_start(out=w2_raw[i][:].rearrange("p t n -> p (t n)"), in_=w2v[:, i, :])
 
-        def op_consts():
-            nc.vector.memset(b2row[:], 0.0)
-            nc.vector.memset(ones[:], 1.0)
-            nc.scalar.dma_start(out=b2row[0:1, :], in_=b2.unsqueeze(0))
-            nc.scalar.dma_start(out=b1t[:].rearrange("p (g t) -> p g t", t=4), in_=b1.rearrange("(g p t) -> p g t", g=NG, t=4))
-            nc.scalar.dma_start(out=padt[:], in_=padding.rearrange("b (q i) -> (b q) i", i=16))
-            make_identity(nc, ident[:])
+        def mask_bias(i):
+            nc.vector.tensor_scalar(out=b2m[:, i, :], in0=b2bc[:], scalar1=keep[:, i:i + 1], scalar2=None, op0=ALU.mult)
 
-        def op_small():
-            nc.vector.tensor_copy(out=b1f[:], in_=b1t[:])
-            nc.vector.tensor_scalar(out=keep[:], in0=padt[:], scalar1=1e-9, scalar2=None, op0=ALU.is_lt)
-
-        def op_b2mm():
-            ps = psum.tile([P, 512], F32, name="b2ps", tag="y3")
-            nc.tensor.matmul(out=ps[:], lhsT=ones[:], rhs=b2row[:], start=True, stop=True)
-            st["b2ps"] = ps
-
-        def op_b2ev(e="S"):
-            copy_on(e, b2bc[:], st["b2ps"][:])
-
-        def op_b2m(i, e="V"):
-            if e == "V":
-                nc.vector.tensor_scalar(out=b2m[:, i, :], in0=b2bc[:], scalar1=keep[:, i:i + 1], scalar2=None, op0=ALU.mult)
-            else:
-                nc.scalar.activation(out=b2m[:, i, :], in_=b2bc[:], func=ACT.Copy, scale=keep[:, i:i + 1])
-
-        def op_xt(tb, h):
+        def x_transpose(tb):
             xw = x_raw[tb][:].bitcast(F32)
-            ps = psum.tile([P, 2, 2, P], F32, name="xps%d" % h, tag="h%d" % h)
-            for a in range(2):
-                for u in range(2):
-                    lo = 256 * (2 * h + a) + 128 * u
-                    nc.tensor.transpose(ps[:, a, u, :], xw[:, lo:lo + 128], ident[:])
-            st["xps", tb, h] = ps
+            for h in range(2):
+                ps = psum.tile([P, 2, 2, P], F32, name="xps", tag="h", bufs=4)
+                for a in range(2):
+                    for u in range(2):
+                        lo = 256 * (2 * h + a) + 128 * u
+                        nc.tensor.transpose(ps[:, a, u, :], xw[:, lo:lo + 128], ident[:])
+                st["xps", tb, h] = ps
 
-        def op_xe(tb, h, e="S"):
-            if ("xg", tb) not in st:
-                st["xg", tb] = work.tile([P, 2048], BF16, name="xg", tag="xg", bufs=2, align_bytes=64)
+        def x_copy(tb):
+            st["xg", tb] = work.tile([P, 2048], BF16, name="xg", tag="xg", bufs=2, align_bytes=64)
             gw = st["xg", tb][:].bitcast(F32).rearrange("p (h a r u) -> p h a r u", h=2, a=2, u=2)
-            copy_on(e, gw[:, h], st["xps", tb, h][:].rearrange("p a u r -> p a r u"))
+            for h in range(2):
+                nc.scalar.copy(out=gw[:, h], in_=st["xps", tb, h][:].rearrange("p a u r -> p a r u"))
 
-        def op_xq(tb):
+        def x_quant(tb):
             nc.vector.quantize_mx(out=xc[:, tb, :].bitcast(FP8X4), scales=xs[:, tb, :], in_=st["xg", tb][:])
 
-        def op_w1rg(g, e="V"):
+        def w1_regroup(g, e):
             t = work.tile([P, 2048], BF16, name="w1g", tag="w1g", bufs=2, align_bytes=64)
             copy_on(e, t[:].rearrange("p (t m j) -> p t m j", t=4, j=4),
                     w1_raw[g][:].rearrange("p j (m t) -> p t m j", t=4))
             st["w1g", g] = t
 
-        def op_w1q(g):
+        def w1_quant(g):
             nc.vector.quantize_mx(out=w1c[:, g, :].bitcast(FP8X4), scales=w1s[:, g, :], in_=st["w1g", g][:])
 
         def regroup(e, dst, src):
             copy_on(e, dst.rearrange("p (c i t) -> p c t i", i=4, t=4), src.rearrange("p t (c i) -> p c t i", i=4))
 
-        def op_w2rg(g, e="V"):
+        def w2_regroup(g):
             t = work.tile([P, 2048], BF16, name="w2g", tag="w2g", bufs=2, align_bytes=64)
-            regroup(e, t[:], w2_raw[g][:])
+            regroup("V", t[:], w2_raw[g][:])
             st["w2g", g] = t
 
-        def op_w2q(g):
+        def w2_quant(g):
             nc.vector.quantize_mx(out=w2c[:, g, :].bitcast(FP8X4), scales=w2s[:, g, :], in_=st["w2g", g][:])
 
-        def op_s1(u, t):
+        def parts(u):
+            return ((0, 256), (256, 512)) if u in SPLIT else ((0, 512),)
+
+        def stage1(u):
             tb, g = divmod(u, NG)
-            ps = psum.tile([P, 512], F32, name="hps%d" % t, tag="h%d" % t)
-            nc.tensor.matmul_mx(out=ps[:], lhsT=w1c[:, g, 128 * t:128 * (t + 1)].bitcast(FP8X4),
-                                lhsT_scale=w1s[:, g, 128 * t:128 * (t + 1)],
-                                rhs=xc[:, tb, :].bitcast(FP8X4), rhs_scale=xs[:, tb, :], start=True, stop=True)
-            st["hps", u, t] = ps
+            banks = []
+            for t in range(4):
+                ps = psum.tile([P, 512], F32, name="hps", tag="h", bufs=4)
+                nc.tensor.matmul_mx(out=ps[:], lhsT=w1c[:, g, 128 * t:128 * (t + 1)].bitcast(FP8X4),
+                                    lhsT_scale=w1s[:, g, 128 * t:128 * (t + 1)],
+                                    rhs=xc[:, tb, :].bitcast(FP8X4), rhs_scale=xs[:, tb, :], start=True, stop=True)
+                banks.append(ps)
+            hp = work.tile([P, 4, 512], BF16, name="hp", tag="hp", bufs=4)
+            for lo, hi in parts(u):
+                for t in range(4):
+                    nc.scalar.activation(out=hp[:, t, lo:hi], in_=banks[t][:, lo:hi], func=ACT.Identity,
+                                         bias=b1f[:, 4 * g + t:4 * g + t + 1], scale=1.0)
+            st["hp", u] = hp
 
-        def cols(hf):
-            return (0, 512) if hf is None else (256 * hf, 256 * (hf + 1))
+        def h_regroup(u, e):
+            hg = work.tile([P, 2048], BF16, name="hg", tag="hg", bufs=3, align_bytes=64)
+            for lo, hi in parts(u):
+                regroup(e, hg[:, 4 * lo:4 * hi], st["hp", u][:, :, lo:hi])
+            st["hg", u] = hg
 
-        def op_ev(u, t, hf=None):
-            g = u % NG
-            if ("hp", u) not in st:
-                st["hp", u] = work.tile([P, 4, 512], BF16, name="hp", tag="hp", bufs=hp_bufs)
-            lo, hi = cols(hf)
-            nc.scalar.activation(out=st["hp", u][:, t, lo:hi], in_=st["hps", u, t][:, lo:hi], func=ACT.Identity,
-                                 bias=b1f[:, 4 * g + t:4 * g + t + 1], scale=1.0)
+        def h_quant(u):
+            hc = work.tile([P, 512], U32, name="hc", tag="hc", bufs=8, align_bytes=64)
+            hs = work.tile([P, 512], U8, name="hs", tag="hs", bufs=8, align_bytes=64)
+            for lo, hi in parts(u):
+                nc.vector.quantize_mx(out=hc[:, lo:hi].bitcast(FP8X4), scales=hs[:, lo:hi], in_=st["hg", u][:, 4 * lo:4 * hi])
+            st["hc", u] = (hc, hs)
 
-        def op_rg(u, hf=None, e="V"):
-            if ("hg", u) not in st:
-                st["hg", u] = work.tile([P, 2048], BF16, name="hg", tag="hg", bufs=hg_bufs, align_bytes=64)
-            lo, hi = cols(hf)
-            regroup(e, st["hg", u][:, 4 * lo:4 * hi], st["hp", u][:, :, lo:hi])
-
-        def op_hq(u, hf=None):
-            if ("hc", u) not in st:
-                st["hc", u] = (work.tile([P, 512], U32, name="hc", tag="hc", bufs=hc_bufs, align_bytes=64),
-                               work.tile([P, 512], U8, name="hs", tag="hs", bufs=hc_bufs, align_bytes=64))
-            hc, hs = st["hc", u]
-            lo, hi = cols(hf)
-            nc.vector.quantize_mx(out=hc[:, lo:hi].bitcast(FP8X4), scales=hs[:, lo:hi], in_=st["hg", u][:, 4 * lo:4 * hi])
-
-        def op_s2(u, a):
+        def stage2(u):
             tb, g = divmod(u, NG)
             hc, hs = st["hc", u]
-            if g == 0:
-                st["y", tb, a] = psum.tile([P, 512], F32, name="yps%d" % a, tag="y%d" % a)
-            nc.tensor.matmul_mx(out=st["y", tb, a][:], lhsT=hc[:, 128 * a:128 * (a + 1)].bitcast(FP8X4),
-                                lhsT_scale=hs[:, 128 * a:128 * (a + 1)],
-                                rhs=w2c[:, g, :].bitcast(FP8X4), rhs_scale=w2s[:, g, :],
-                                start=(g == 0), stop=(g == NG - 1))
+            for a in range(4):
+                if g == 0:
+                    st["y", tb, a] = psum.tile([P, 512], F32, name="yps%d" % a, tag="y%d" % a)
+                nc.tensor.matmul_mx(out=st["y", tb, a][:], lhsT=hc[:, 128 * a:128 * (a + 1)].bitcast(FP8X4),
+                                    lhsT_scale=hs[:, 128 * a:128 * (a + 1)],
+                                    rhs=w2c[:, g, :].bitcast(FP8X4), rhs_scale=w2s[:, g, :],
+                                    start=(g == 0), stop=(g == NG - 1))
 
-        def op_out(tb, a):
-            i = 4 * tb + a
-            ot = work.tile([P, 512], F32, name="ot", tag="ot", bufs=ot_bufs)
-            nc.vector.scalar_tensor_tensor(out=ot[:], in0=st["y", tb, a][:], scalar=keep[:, i:i + 1],
-                                           in1=b2m[:, i, :], op0=ALU.mult, op1=ALU.add)
-            nc.sync.dma_start(out=ov[:, i, :], in_=ot[:])
+        def finish(tb):
+            for a in range(4):
+                i = 4 * tb + a
+                ot = work.tile([P, 512], F32, name="ot", tag="ot", bufs=6)
+                nc.vector.scalar_tensor_tensor(out=ot[:], in0=st["y", tb, a][:], scalar=keep[:, i:i + 1],
+                                               in1=b2m[:, i, :], op0=ALU.mult, op1=ALU.add)
+                nc.sync.dma_start(out=ov[:, i, :], in_=ot[:])
 
-        table = dict(load=op_load, consts=op_consts, small=op_small, b2mm=op_b2mm, b2ev=op_b2ev, b2m=op_b2m,
-                     xt=op_xt, xe=op_xe, xq=op_xq, w1rg=op_w1rg, w1q=op_w1q, w2rg=op_w2rg, w2q=op_w2q,
-                     s1=op_s1, ev=op_ev, rg=op_rg, hq=op_hq, s2=op_s2, out=op_out)
-        for o in sched:
-            table[o[0]](*o[1:])
+        nc.vector.memset(b2row[:], 0.0)
+        nc.vector.memset(ones[:], 1.0)
+        nc.scalar.dma_start(out=b2row[0:1, :], in_=b2.unsqueeze(0))
+        nc.scalar.dma_start(out=b1t[:].rearrange("p (g t) -> p g t", t=4), in_=b1.rearrange("(g p t) -> p g t", g=NG, t=4))
+        nc.scalar.dma_start(out=padt[:], in_=padding.rearrange("b (q i) -> (b q) i", i=16))
+        make_identity(nc, ident[:])
+        for what, i in LOADS:
+            load(what, i)
 
+        nc.vector.tensor_copy(out=b1f[:], in_=b1t[:])
+        nc.vector.tensor_scalar(out=keep[:], in0=padt[:], scalar1=1e-9, scalar2=None, op0=ALU.is_lt)
+        b2ps = psum.tile([P, 512], F32, name="b2ps", tag="y3")
+        nc.tensor.matmul(out=b2ps[:], lhsT=ones[:], rhs=b2row[:], start=True, stop=True)
+        nc.scalar.copy(out=b2bc[:], in_=b2ps[:])
+        w1_regroup(0, "V")
+        mask_bias(0)
+        mask_bias(1)
+        w1_quant(0)
+        x_transpose(0)
+        x_copy(0)
+        for i in (2, 3, 4):
+            mask_bias(i)
+        x_quant(0)
+        w1_regroup(1, "S")
+        w1_regroup(2, "S")
+        w2_regroup(0)
+        mask_bias(5)
+        mask_bias(6)
+        w2_quant(0)
+        w1_quant(1)
+        w2_regroup(1)
+        w1_regroup(3, "V")
+        w1_quant(2)
+        w1_quant(3)
+        w2_quant(1)
+        w2_regroup(2)
+        w2_regroup(3)
+        w2_quant(2)
 
-LOADS = [("w1", 0), ("x", 0), ("w1", 1), ("w2", 0), ("w1", 2), ("w2", 1), ("w1", 3), ("w2", 2), ("x", 1), ("w2", 3),
-         ("x", 2), ("x", 3)]
-ON_SCALAR = (("w1", 1), ("w1", 2))
-
-
-def natural():
-    s = [("consts",)] + [("load",) + l for l in LOADS] + [("small",), ("b2mm",), ("b2ev", "S")]
-
-    def wprep(w, g):
-        e = "S" if (w, g) in ON_SCALAR else "V"
-        return [(w + "rg", g, e), (w + "q", g)]
-
-    def xprep(tb):
-        return [("xt", tb, 0), ("xt", tb, 1), ("xe", tb, 0, "S"), ("xe", tb, 1, "S"), ("xq", tb)]
-
-    s += wprep("w1", 0) + xprep(0)
-    for u in range(16):
-        tb, g = divmod(u, 4)
-        s += [("s1", u, t) for t in range(4)]
-        if tb == 0 and g < 3:
-            s += wprep("w1", g + 1)
-        s += [("ev", u, t, None) for t in range(4)]
-        if g == 1 and tb < 3:
-            s += xprep(tb + 1)
-        if tb == 0:
-            s += wprep("w2", g)
-        s += [("rg", u, None, "V"), ("hq", u, None)]
-        if g == 2:
-            s += [("b2m", 4 * tb + a, "V") for a in range(4)]
-        s += [("s2", u, a) for a in range(4)]
-        if g == 3:
-            s += [("out", tb, a) for a in range(4)]
-    return s
-
-
-def tile_feedforwardnetwork_kernel(tc, x, padding, filter_weight, filter_bias, output_weight, output_bias, out):
-    build(tc, x, padding, filter_weight, filter_bias, output_weight, output_bias, out, natural(), manual=False)
+        todo = list(range(7, 16))
+        for u in range(NU + LAG2 + 1):
+            if u < NU:
+                stage1(u)
+                if u in RG_ON_SCALAR:
+                    h_regroup(u, "S")
+                if u % 4 == 1 and u < 12:
+                    x_transpose(u // 4 + 1)
+                    x_copy(u // 4 + 1)
+            if 0 <= u - LAG2 < NU:
+                stage2(u - LAG2)
+            v = u - 1
+            if 0 <= v < NU:
+                if v not in RG_ON_SCALAR:
+                    h_regroup(v, "V")
+                if v == 0:
+                    x_quant(1)
+                    w2_quant(3)
+                elif v % 4 == 1 and 5 <= v < 12:
+                    x_quant(v // 4 + 1)
+                elif v % 4 == 2 and v >= 6:
+                    finish((v - 6) // 4)
+                elif len(todo) > 0:
+                    mask_bias(todo[0])
+                    todo = todo[1:]
+                h_quant(v)
+        finish(NTB - 1)

@@ -20,7 +20,7 @@ NU = NTB * NG
 LAG2 = 4
 LOADS = (("w1", 0), ("x", 0), ("w1", 1), ("w2", 0), ("w1", 2), ("w2", 1), ("w1", 3), ("w2", 2), ("x", 1), ("w2", 3),
          ("x", 2), ("x", 3))
-RG_ON_SCALAR = (14,)
+RG_ON_SCALAR = ()
 SPLIT = (15,)
 
 

@@ -20,14 +20,13 @@ NU = NTB * NG
 LAG2 = 4
 LOADS = (("w1", 0), ("x", 0), ("w1", 1), ("w2", 0), ("w1", 2), ("w2", 1), ("w1", 3), ("w2", 2), ("x", 1), ("w2", 3),
          ("x", 2), ("x", 3))
-RG_ON_SCALAR = ()
+RG_ON_SCALAR = (14,)
 SPLIT = (15,)
 
 
 def tile_feedforwardnetwork_kernel(tc, x, padding, w1, b1, w2, b2, out):
     nc = tc.nc
     with ExitStack() as ctx:
-        ctx.enter_context(tc.manual_schedule())
         const = ctx.enter_context(tc.tile_pool(name="const", bufs=1))
         raw = ctx.enter_context(tc.tile_pool(name="raw", bufs=1))
         work = ctx.enter_context(tc.tile_pool(name="work", bufs=1))

from contextlib import ExitStack

import concourse.mybir as mybir
from concourse.masks import make_identity

FLOPS = 2 * 2048 * 512 * 2048 * 2

F32 = mybir.dt.float32
BF16 = mybir.dt.bfloat16
U32 = mybir.dt.uint32
U8 = mybir.dt.uint8
FP8X4 = mybir.dt.float8_e4m3fn_x4
ALU = mybir.AluOpType
ACT = mybir.ActivationFunctionType

P = 128
NTB = 4
NG = 4
NU = NTB * NG
LAG2 = 4
LOADS = (("w1", 0), ("x", 0), ("w1", 1), ("w2", 0), ("w1", 2), ("w2", 1), ("w1", 3), ("w2", 2), ("x", 1), ("w2", 3),
         ("x", 2), ("x", 3))
RG_ON_SCALAR = (14,)
SPLIT = (15,)


def tile_feedforwardnetwork_kernel(tc, x, padding, w1, b1, w2, b2, out):
    nc = tc.nc
    with ExitStack() as ctx:
        const = ctx.enter_context(tc.tile_pool(name="const", bufs=1))
        raw = ctx.enter_context(tc.tile_pool(name="raw", bufs=1))
        work = ctx.enter_context(tc.tile_pool(name="work", bufs=1))
        psum = ctx.enter_context(tc.psum_pool(name="psum", bufs=1))

        xv = x.flatten_outer_dims().rearrange("(p i) k -> p (i k)", i=16)
        ov = out.flatten_outer_dims().rearrange("(p i) n -> p i n", i=16)
        w1v = w1.rearrange("(u q e) f -> q u e f", u=2, e=2)
        w2v = w2.rearrange("(g p t) n -> p g (t n)", g=NG, t=4)

        x_raw = [raw.tile([P, 2048], BF16, name="x_raw%d" % i) for i in range(NTB)]
        w1_raw = [raw.tile([P, 4, 512], BF16, name="w1_raw%d" % i) for i in range(NG)]
        w2_raw = [raw.tile([P, 4, 512], BF16, name="w2_raw%d" % i) for i in range(NG)]

        xc = const.tile([P, NTB, 512], U32, name="xc", align_bytes=64)
        xs = const.tile([P, NTB, 512], U8, name="xs", align_bytes=64)
        w1c = const.tile([P, NG, 512], U32, name="w1c", align_bytes=64)
        w1s = const.tile([P, NG, 512], U8, name="w1s", align_bytes=64)
        w2c = const.tile([P, NG, 512], U32, name="w2c", align_bytes=64)
        w2s = const.tile([P, NG, 512], U8, name="w2s", align_bytes=64)

        ident = const.tile([P, P], F32, name="ident")
        ones = const.tile([P, P], BF16, name="ones")
        b2row = const.tile([P, 512], BF16, name="b2row")
        b2bc = const.tile([P, 512], BF16, name="b2bc")
        b2m = const.tile([P, 16, 512], BF16, name="b2m")
        b1t = const.tile([P, 16], BF16, name="b1t")
        b1f = const.tile([P, 16], F32, name="b1f")
        padt = const.tile([P, 16], BF16, name="padt")
        keep = const.tile([P, 16], F32, name="keep")

        st = {}

        def copy_on(e, dst, src):
            if e == "S":
                nc.scalar.copy(out=dst, in_=src)
            else:
                nc.vector.tensor_copy(out=dst, in_=src)

        def load(what, i):
            if what == "x":
                nc.sync.dma_start(out=x_raw[i][:], in_=xv[:, 2048 * i:2048 * (i + 1)])
            elif what == "w1":
                for u in range(2):
                    nc.sync.dma_start(out=w1_raw[i][:, 2 * u:2 * u + 2, :], in_=w1v[:, u, :, 512 * i:512 * (i + 1)])
            else:
                nc.sync.dma_start(out=w2_raw[i][:].rearrange("p t n -> p (t n)"), in_=w2v[:, i, :])

        def mask_bias(i):
            nc.vector.tensor_scalar(out=b2m[:, i, :], in0=b2bc[:], scalar1=keep[:, i:i + 1], scalar2=None, op0=ALU.mult)

        def x_transpose(tb):
            xw = x_raw[tb][:].bitcast(F32)
            for h in range(2):
                ps = psum.tile([P, 2, 2, P], F32, name="xps", tag="h", bufs=4)
                for a in range(2):
                    for u in range(2):
                        lo = 256 * (2 * h + a) + 128 * u
                        nc.tensor.transpose(ps[:, a, u, :], xw[:, lo:lo + 128], ident[:])
                st["xps", tb, h] = ps

        def x_copy(tb):
            st["xg", tb] = work.tile([P, 2048], BF16, name="xg", tag="xg", bufs=2, align_bytes=64)
            gw = st["xg", tb][:].bitcast(F32).rearrange("p (h a r u) -> p h a r u", h=2, a=2, u=2)
            for h in range(2):
                nc.scalar.copy(out=gw[:, h], in_=st["xps", tb, h][:].rearrange("p a u r -> p a r u"))

        def x_quant(tb):
            nc.vector.quantize_mx(out=xc[:, tb, :].bitcast(FP8X4), scales=xs[:, tb, :], in_=st["xg", tb][:])

        def w1_regroup(g, e):
            t = work.tile([P, 2048], BF16, name="w1g", tag="w1g", bufs=2, align_bytes=64)
            copy_on(e, t[:].rearrange("p (t m j) -> p t m j", t=4, j=4),
                    w1_raw[g][:].rearrange("p j (m t) -> p t m j", t=4))
            st["w1g", g] = t

        def w1_quant(g):
            nc.vector.quantize_mx(out=w1c[:, g, :].bitcast(FP8X4), scales=w1s[:, g, :], in_=st["w1g", g][:])

        def regroup(e, dst, src):
            copy_on(e, dst.rearrange("p (c i t) -> p c t i", i=4, t=4), src.rearrange("p t (c i) -> p c t i", i=4))

        def w2_regroup(g):
            t = work.tile([P, 2048], BF16, name="w2g", tag="w2g", bufs=2, align_bytes=64)
            regroup("V", t[:], w2_raw[g][:])
            st["w2g", g] = t

        def w2_quant(g):
            nc.vector.quantize_mx(out=w2c[:, g, :].bitcast(FP8X4), scales=w2s[:, g, :], in_=st["w2g", g][:])

        def parts(u):
            return ((0, 256), (256, 512)) if u in SPLIT else ((0, 512),)

        def stage1(u):
            tb, g = divmod(u, NG)
            banks = []
            for t in range(4):
                ps = psum.tile([P, 512], F32, name="hps", tag="h", bufs=4)
                nc.tensor.matmul_mx(out=ps[:], lhsT=w1c[:, g, 128 * t:128 * (t + 1)].bitcast(FP8X4),
                                    lhsT_scale=w1s[:, g, 128 * t:128 * (t + 1)],
                                    rhs=xc[:, tb, :].bitcast(FP8X4), rhs_scale=xs[:, tb, :], start=True, stop=True)
                banks.append(ps)
            hp = work.tile([P, 4, 512], BF16, name="hp", tag="hp", bufs=4)
            for lo, hi in parts(u):
                for t in range(4):
                    nc.scalar.activation(out=hp[:, t, lo:hi], in_=banks[t][:, lo:hi], func=ACT.Identity,
                                         bias=b1f[:, 4 * g + t:4 * g + t + 1], scale=1.0)
            st["hp", u] = hp

        def h_regroup(u, e):
            hg = work.tile([P, 2048], BF16, name="hg", tag="hg", bufs=3, align_bytes=64)
            for lo, hi in parts(u):
                regroup(e, hg[:, 4 * lo:4 * hi], st["hp", u][:, :, lo:hi])
            st["hg", u] = hg

        def h_quant(u):
            hc = work.tile([P, 512], U32, name="hc", tag="hc", bufs=8, align_bytes=64)
            hs = work.tile([P, 512], U8, name="hs", tag="hs", bufs=8, align_bytes=64)
            for lo, hi in parts(u):
                nc.vector.quantize_mx(out=hc[:, lo:hi].bitcast(FP8X4), scales=hs[:, lo:hi], in_=st["hg", u][:, 4 * lo:4 * hi])
            st["hc", u] = (hc, hs)

        def stage2(u):
            tb, g = divmod(u, NG)
            hc, hs = st["hc", u]
            for a in range(4):
                if g == 0:
                    st["y", tb, a] = psum.tile([P, 512], F32, name="yps%d" % a, tag="y%d" % a)
                nc.tensor.matmul_mx(out=st["y", tb, a][:], lhsT=hc[:, 128 * a:128 * (a + 1)].bitcast(FP8X4),
                                    lhsT_scale=hs[:, 128 * a:128 * (a + 1)],
                                    rhs=w2c[:, g, :].bitcast(FP8X4), rhs_scale=w2s[:, g, :],
                                    start=(g == 0), stop=(g == NG - 1))

        def finish(tb):
            for a in range(4):
                i = 4 * tb + a
                ot = work.tile([P, 512], F32, name="ot", tag="ot", bufs=6)
                nc.vector.scalar_tensor_tensor(out=ot[:], in0=st["y", tb, a][:], scalar=keep[:, i:i + 1],
                                               in1=b2m[:, i, :], op0=ALU.mult, op1=ALU.add)
                nc.sync.dma_start(out=ov[:, i, :], in_=ot[:])

        nc.vector.memset(b2row[:], 0.0)
        nc.vector.memset(ones[:], 1.0)
        nc.scalar.dma_start(out=b2row[0:1, :], in_=b2.unsqueeze(0))
        nc.scalar.dma_start(out=b1t[:].rearrange("p (g t) -> p g t", t=4), in_=b1.rearrange("(g p t) -> p g t", g=NG, t=4))
        nc.scalar.dma_start(out=padt[:], in_=padding.rearrange("b (q i) -> (b q) i", i=16))
        make_identity(nc, ident[:])
        for what, i in LOADS:
            load(what, i)

        nc.vector.tensor_copy(out=b1f[:], in_=b1t[:])
        nc.vector.tensor_scalar(out=keep[:], in0=padt[:], scalar1=1e-9, scalar2=None, op0=ALU.is_lt)
        b2ps = psum.tile([P, 512], F32, name="b2ps", tag="y3")
        nc.tensor.matmul(out=b2ps[:], lhsT=ones[:], rhs=b2row[:], start=True, stop=True)
        nc.scalar.copy(out=b2bc[:], in_=b2ps[:])
        w1_regroup(0, "V")
        mask_bias(0)
        mask_bias(1)
        w1_quant(0)
        x_transpose(0)
        x_copy(0)
        for i in (2, 3, 4):
            mask_bias(i)
        x_quant(0)
        w1_regroup(1, "S")
        w1_regroup(2, "S")
        w2_regroup(0)
        mask_bias(5)
        mask_bias(6)
        w2_quant(0)
        w1_quant(1)
        w2_regroup(1)
        w1_regroup(3, "V")
        w1_quant(2)
        w1_quant(3)
        w2_quant(1)
        w2_regroup(2)
        w2_regroup(3)
        w2_quant(2)

        todo = list(range(7, 16))
        for u in range(NU + LAG2 + 1):
            if u < NU:
                stage1(u)
                if u in RG_ON_SCALAR:
                    h_regroup(u, "S")
                if u % 4 == 1 and u < 12:
                    x_transpose(u // 4 + 1)
                    x_copy(u // 4 + 1)
            if 0 <= u - LAG2 < NU:
                stage2(u - LAG2)
            v = u - 1
            if 0 <= v < NU:
                if v not in RG_ON_SCALAR:
                    h_regroup(v, "V")
                if v == 0:
                    x_quant(1)
                    w2_quant(3)
                elif v % 4 == 1 and 5 <= v < 12:
                    x_quant(v // 4 + 1)
                elif v % 4 == 2 and v >= 6:
                    finish((v - 6) // 4)
                elif len(todo) > 0:
                    mask_bias(todo[0])
                    todo = todo[1:]
                h_quant(v)
        finish(NTB - 1)
